import numpy as np
import ml_dtypes

BF16 = ml_dtypes.bfloat16


def bf(x):
    return np.asarray(x, np.float32).astype(BF16)


def f32(x):
    return np.asarray(x, np.float32)


def f64(x):
    return np.asarray(x).astype(np.float64)


def striped(idx):
    return np.tile(idx.reshape(-1, 16).T, (8, 1))


S, D, H, N, MM = 256, 128, 256, 64, 128


def setup_inputs():
    return {
        "table": bf(np.random.standard_normal((S, D))),
        "wj": bf(np.random.standard_normal((D, H)) / np.sqrt(2.0 * D)),
        "fm": bf(np.random.standard_normal((D, MM))),
        "wm": bf(np.random.standard_normal((D, H)) / np.sqrt(2.0 * D)),
        "b": f32(0.1 * np.random.standard_normal((H, 1))),
        "offs": striped(np.random.permutation(S)[:N]),
    }


def reference(table, wj, fm, wm, b, offs):
    idx = offs[:16].T.reshape(-1)
    a = f64(wj).T @ f64(table)[idx].T + f64(b)
    u = f64(wm).T @ f64(fm)
    return np.tanh(a[:, :, None] + u[:, None, :]).reshape(H, N * MM)

@@ -1,0 +1,69 @@
+import concourse.mybir as mybir
+from concourse.masks import make_identity
+
+BF16, F32, U16 = mybir.dt.bfloat16, mybir.dt.float32, mybir.dt.uint16
+TANH = mybir.ActivationFunctionType.Tanh
+
+P = 128
+S = 256
+H = 256
+N = 64
+M = 128
+J = 8
+
+FLOPS = 2 * P * H * (N + M)
+
+
+def tile_learnablenetwork_kernel(tc, table, wj, fm, wm, b, offs, out):
+    nc = tc.nc
+    with (
+        tc.tile_pool(name="held", bufs=1) as held,
+        tc.tile_pool(name="staged", bufs=(H // P) * (N // J)) as staged,
+        tc.psum_pool(name="psum", bufs=1) as psum,
+    ):
+        offsets = held.tile([P, N // 16], U16, name="offsets")
+        rows = held.tile([P, S // P, P], BF16, name="rows")
+        wj_sb = held.tile([P, H], BF16, name="wj_sb")
+        wm_sb = held.tile([P, H], BF16, name="wm_sb")
+        fm_sb = held.tile([P, M], BF16, name="fm_sb")
+        nc.sync.dma_start(rows[:], table.rearrange("(k p) d -> p k d", p=P))
+        nc.sync.dma_start(offsets[:], offs)
+        nc.scalar.dma_start(wm_sb[:], wm)
+        nc.scalar.dma_start(fm_sb[:], fm)
+        nc.scalar.dma_start(wj_sb[:], wj)
+        bias = [held.tile([P, 1], F32, name=f"bias{k}") for k in range(H // P)]
+        for k in range(H // P):
+            nc.sync.dma_start(bias[k][:], b[k * P : (k + 1) * P, :])
+
+        identity = held.tile([P, P], BF16, name="identity")
+        make_identity(nc, identity[:])
+        turned = psum.tile([P, S], BF16, name="turned")
+        for k in range(S // P):
+            nc.tensor.transpose(turned[:, k * P : (k + 1) * P], rows[:, k, :], identity[:])
+        window = held.tile([P, S], BF16, name="window")
+        nc.vector.tensor_copy(window[:], turned[:])
+
+        cand = []
+        mach = []
+        for k in range(H // P):
+            mach_ps = psum.tile([P, M], F32, name=f"mach_ps{k}")
+            nc.tensor.matmul(mach_ps[:], wm_sb[:, k * P : (k + 1) * P], fm_sb[:])
+            mach_k = held.tile([P, M], F32, name=f"mach{k}")
+            nc.vector.tensor_scalar_add(mach_k[:], mach_ps[:], bias[k][:, 0:1])
+            mach.append(mach_k)
+        for k in range(H // P):
+            cand_ps = psum.tile([P, N], F32, name=f"cand_ps{k}")
+            nc.tensor.matmul(cand_ps[:], wj_sb[:, k * P : (k + 1) * P], window[:].indirect(offsets[:]))
+            cand_k = held.tile([P, N], F32, name=f"cand{k}")
+            nc.vector.tensor_copy(cand_k[:], cand_ps[:])
+            cand.append(cand_k)
+
+        for k in range(H // P):
+            for c in range(N // J):
+                pairs = staged.tile([P, J * M], F32, name="pairs")
+                for i in range(J):
+                    j = c * J + i
+                    nc.scalar.activation(
+                        pairs[:, i * M : (i + 1) * M], mach[k][:], TANH, bias=cand[k][:, j : j + 1]
+                    )
+                nc.sync.dma_start(out[k * P : (k + 1) * P, c * J * M : (c + 1) * J * M], pairs[:])

@@ -63,7 +63,6 @@ def tile_learnablenetwork_kernel(tc, table, wj, fm, wm, b, offs, out):
                 pairs = staged.tile([P, J * M], F32, name="pairs")
                 for i in range(J):
                     j = c * J + i
-                    nc.scalar.activation(
-                        pairs[:, i * M : (i + 1) * M], mach[k][:], TANH, bias=cand[k][:, j : j + 1]
-                    )
+                    nc.vector.tensor_scalar_add(pairs[:, i * M : (i + 1) * M], mach[k][:], cand[k][:, j : j + 1])
+                nc.scalar.activation(pairs[:], pairs[:], TANH)
                 nc.sync.dma_start(out[k * P : (k + 1) * P, c * J * M : (c + 1) * J * M], pairs[:])

@@ -63,6 +63,11 @@ def tile_learnablenetwork_kernel(tc, table, wj, fm, wm, b, offs, out):
                 pairs = staged.tile([P, J * M], F32, name="pairs")
                 for i in range(J):
                     j = c * J + i
-                    nc.vector.tensor_scalar_add(pairs[:, i * M : (i + 1) * M], mach[k][:], cand[k][:, j : j + 1])
-                nc.scalar.activation(pairs[:], pairs[:], TANH)
+                    one = pairs[:, i * M : (i + 1) * M]
+                    if k == 0 and c == 0:
+                        nc.scalar.activation(one, mach[k][:], TANH, bias=cand[k][:, j : j + 1])
+                    else:
+                        nc.vector.tensor_scalar_add(one, mach[k][:], cand[k][:, j : j + 1])
+                if not (k == 0 and c == 0):
+                    nc.scalar.activation(pairs[:], pairs[:], TANH)
                 nc.sync.dma_start(out[k * P : (k + 1) * P, c * J * M : (c + 1) * J * M], pairs[:])

@@ -9,7 +9,7 @@ S = 256
 H = 256
 N = 64
 M = 128
-J = 8
+DIRECT = 6
 
 FLOPS = 2 * P * H * (N + M)
 
@@ -18,7 +18,7 @@ def tile_learnablenetwork_kernel(tc, table, wj, fm, wm, b, offs, out):
     nc = tc.nc
     with (
         tc.tile_pool(name="held", bufs=1) as held,
-        tc.tile_pool(name="staged", bufs=(H // P) * (N // J)) as staged,
+        tc.tile_pool(name="staged", bufs=1) as staged,
         tc.psum_pool(name="psum", bufs=1) as psum,
     ):
         offsets = held.tile([P, N // 16], U16, name="offsets")
@@ -58,16 +58,21 @@ def tile_learnablenetwork_kernel(tc, table, wj, fm, wm, b, offs, out):
             nc.vector.tensor_copy(cand_k[:], cand_ps[:])
             cand.append(cand_k)
 
+        width = 1
         for k in range(H // P):
-            for c in range(N // J):
-                pairs = staged.tile([P, J * M], F32, name="pairs")
-                for i in range(J):
-                    j = c * J + i
+            first = 0
+            while first < N:
+                count = min(width, N - first)
+                pairs = staged.tile([P, count * M], F32, name=f"pairs{k}_{first}")
+                for i in range(count):
+                    j = first + i
                     one = pairs[:, i * M : (i + 1) * M]
-                    if k == 0 and c == 0:
+                    if k == 0 and first < DIRECT:
                         nc.scalar.activation(one, mach[k][:], TANH, bias=cand[k][:, j : j + 1])
                     else:
                         nc.vector.tensor_scalar_add(one, mach[k][:], cand[k][:, j : j + 1])
-                if not (k == 0 and c == 0):
+                if not (k == 0 and first < DIRECT):
                     nc.scalar.activation(pairs[:], pairs[:], TANH)
-                nc.sync.dma_start(out[k * P : (k + 1) * P, c * J * M : (c + 1) * J * M], pairs[:])
+                nc.sync.dma_start(out[k * P : (k + 1) * P, first * M : (first + count) * M], pairs[:])
+                first += count
+                width += 1

@@ -43,20 +43,16 @@ def tile_learnablenetwork_kernel(tc, table, wj, fm, wm, b, offs, out):
         window = held.tile([P, S], BF16, name="window")
         nc.vector.tensor_copy(window[:], turned[:])
 
-        cand = []
-        mach = []
+        cand_ps = [psum.tile([P, N], F32, name=f"cand_ps{k}") for k in range(H // P)]
+        mach_ps = [psum.tile([P, M], F32, name=f"mach_ps{k}") for k in range(H // P)]
+        cand = [held.tile([P, N], F32, name=f"cand{k}") for k in range(H // P)]
+        mach = [held.tile([P, M], F32, name=f"mach{k}") for k in range(H // P)]
+        nc.tensor.matmul(mach_ps[0][:], wm_sb[:, 0:P], fm_sb[:])
         for k in range(H // P):
-            mach_ps = psum.tile([P, M], F32, name=f"mach_ps{k}")
-            nc.tensor.matmul(mach_ps[:], wm_sb[:, k * P : (k + 1) * P], fm_sb[:])
-            mach_k = held.tile([P, M], F32, name=f"mach{k}")
-            nc.vector.tensor_scalar_add(mach_k[:], mach_ps[:], bias[k][:, 0:1])
-            mach.append(mach_k)
-        for k in range(H // P):
-            cand_ps = psum.tile([P, N], F32, name=f"cand_ps{k}")
-            nc.tensor.matmul(cand_ps[:], wj_sb[:, k * P : (k + 1) * P], window[:].indirect(offsets[:]))
-            cand_k = held.tile([P, N], F32, name=f"cand{k}")
-            nc.vector.tensor_copy(cand_k[:], cand_ps[:])
-            cand.append(cand_k)
+            nc.tensor.matmul(cand_ps[k][:], wj_sb[:, k * P : (k + 1) * P], window[:].indirect(offsets[:]))
+        nc.tensor.matmul(mach_ps[1][:], wm_sb[:, P : 2 * P], fm_sb[:])
+        nc.scalar.copy(mach[0][:], mach_ps[0][:])
+        nc.vector.tensor_scalar_add(cand[0][:], cand_ps[0][:], bias[0][:, 0:1])
 
         width = 1
         for k in range(H // P):
@@ -74,5 +70,8 @@ def tile_learnablenetwork_kernel(tc, table, wj, fm, wm, b, offs, out):
                 if not (k == 0 and first < DIRECT):
                     nc.scalar.activation(pairs[:], pairs[:], TANH)
                 nc.sync.dma_start(out[k * P : (k + 1) * P, first * M : (first + count) * M], pairs[:])
+                if k == 0 and first == DIRECT:
+                    nc.vector.tensor_copy(mach[1][:], mach_ps[1][:])
+                    nc.vector.tensor_scalar_add(cand[1][:], cand_ps[1][:], bias[1][:, 0:1])
                 first += count
                 width += 1

@@ -54,11 +54,11 @@ def tile_learnablenetwork_kernel(tc, table, wj, fm, wm, b, offs, out):
         nc.scalar.copy(mach[0][:], mach_ps[0][:])
         nc.vector.tensor_scalar_add(cand[0][:], cand_ps[0][:], bias[0][:, 0:1])
 
-        width = 1
+        stores = 0
         for k in range(H // P):
             first = 0
             while first < N:
-                count = min(width, N - first)
+                count = min(1 + stores // 2, N - first)
                 pairs = staged.tile([P, count * M], F32, name=f"pairs{k}_{first}")
                 for i in range(count):
                     j = first + i
@@ -74,4 +74,4 @@ def tile_learnablenetwork_kernel(tc, table, wj, fm, wm, b, offs, out):
                     nc.vector.tensor_copy(mach[1][:], mach_ps[1][:])
                     nc.vector.tensor_scalar_add(cand[1][:], cand_ps[1][:], bias[1][:, 0:1])
                 first += count
-                width += 1
+                stores += 1

@@ -27,10 +27,10 @@ def tile_learnablenetwork_kernel(tc, table, wj, fm, wm, b, offs, out):
         wm_sb = held.tile([P, H], BF16, name="wm_sb")
         fm_sb = held.tile([P, M], BF16, name="fm_sb")
         nc.sync.dma_start(rows[:], table.rearrange("(k p) d -> p k d", p=P))
+        nc.sync.dma_start(wm_sb[:], wm)
+        nc.sync.dma_start(fm_sb[:], fm)
         nc.sync.dma_start(offsets[:], offs)
-        nc.scalar.dma_start(wm_sb[:], wm)
-        nc.scalar.dma_start(fm_sb[:], fm)
-        nc.scalar.dma_start(wj_sb[:], wj)
+        nc.sync.dma_start(wj_sb[:], wj)
         bias = [held.tile([P, 1], F32, name=f"bias{k}") for k in range(H // P)]
         for k in range(H // P):
             nc.sync.dma_start(bias[k][:], b[k * P : (k + 1) * P, :])

@@ -59,7 +59,7 @@ def tile_learnablenetwork_kernel(tc, table, wj, fm, wm, b, offs, out):
             first = 0
             while first < N:
                 count = min(1 + stores // 2, N - first)
-                pairs = staged.tile([P, count * M], F32, name=f"pairs{k}_{first}")
+                pairs = staged.tile([P, count * M], F32, name=f"pairs{k}_{first}", align_bytes=256)
                 for i in range(count):
                     j = first + i
                     one = pairs[:, i * M : (i + 1) * M]

@@ -60,13 +60,18 @@ def tile_learnablenetwork_kernel(tc, table, wj, fm, wm, b, offs, out):
             while first < N:
                 count = min(1 + stores // 2, N - first)
                 pairs = staged.tile([P, count * M], F32, name=f"pairs{k}_{first}", align_bytes=256)
-                for i in range(count):
-                    j = first + i
-                    one = pairs[:, i * M : (i + 1) * M]
-                    if k == 0 and first < DIRECT:
-                        nc.scalar.activation(one, mach[k][:], TANH, bias=cand[k][:, j : j + 1])
-                    else:
-                        nc.vector.tensor_scalar_add(one, mach[k][:], cand[k][:, j : j + 1])
+                if k == 0:
+                    for i in range(count):
+                        j = first + i
+                        one = pairs[:, i * M : (i + 1) * M]
+                        if first < DIRECT:
+                            nc.scalar.activation(one, mach[k][:], TANH, bias=cand[k][:, j : j + 1])
+                        else:
+                            nc.vector.tensor_scalar_add(one, mach[k][:], cand[k][:, j : j + 1])
+                else:
+                    machines = mach[k][:].unsqueeze(1).to_broadcast([P, count, M])
+                    candidates = cand[k][:, first : first + count].unsqueeze(2).to_broadcast([P, count, M])
+                    nc.vector.tensor_add(pairs[:].rearrange("p (c m) -> p c m", m=M), machines, candidates)
                 if not (k == 0 and first < DIRECT):
                     nc.scalar.activation(pairs[:], pairs[:], TANH)
                 nc.sync.dma_start(out[k * P : (k + 1) * P, first * M : (first + count) * M], pairs[:])

@@ -51,8 +51,8 @@ def tile_learnablenetwork_kernel(tc, table, wj, fm, wm, b, offs, out):
         for k in range(H // P):
             nc.tensor.matmul(cand_ps[k][:], wj_sb[:, k * P : (k + 1) * P], window[:].indirect(offsets[:]))
         nc.tensor.matmul(mach_ps[1][:], wm_sb[:, P : 2 * P], fm_sb[:])
-        nc.scalar.copy(mach[0][:], mach_ps[0][:])
         nc.vector.tensor_scalar_add(cand[0][:], cand_ps[0][:], bias[0][:, 0:1])
+        nc.vector.tensor_copy(mach[0][:], mach_ps[0][:])
 
         stores = 0
         for k in range(H // P):
@@ -65,7 +65,7 @@ def tile_learnablenetwork_kernel(tc, table, wj, fm, wm, b, offs, out):
                         j = first + i
                         one = pairs[:, i * M : (i + 1) * M]
                         if first < DIRECT:
-                            nc.scalar.activation(one, mach[k][:], TANH, bias=cand[k][:, j : j + 1])
+                            nc.scalar.activation(one, mach_ps[k][:], TANH, bias=cand[k][:, j : j + 1])
                         else:
                             nc.vector.tensor_scalar_add(one, mach[k][:], cand[k][:, j : j + 1])
                 else:

@@ -26,7 +26,8 @@ def tile_learnablenetwork_kernel(tc, table, wj, fm, wm, b, offs, out):
         wj_sb = held.tile([P, H], BF16, name="wj_sb")
         wm_sb = held.tile([P, H], BF16, name="wm_sb")
         fm_sb = held.tile([P, M], BF16, name="fm_sb")
-        nc.sync.dma_start(rows[:], table.rearrange("(k p) d -> p k d", p=P))
+        for k in range(S // P):
+            nc.sync.dma_start(rows[:, k, :], table[k * P : (k + 1) * P, :])
         nc.sync.dma_start(wm_sb[:], wm)
         nc.sync.dma_start(fm_sb[:], fm)
         nc.sync.dma_start(offsets[:], offs)
@@ -37,14 +38,18 @@ def tile_learnablenetwork_kernel(tc, table, wj, fm, wm, b, offs, out):
 
         identity = held.tile([P, P], BF16, name="identity")
         make_identity(nc, identity[:])
-        turned = psum.tile([P, S], BF16, name="turned")
-        for k in range(S // P):
-            nc.tensor.transpose(turned[:, k * P : (k + 1) * P], rows[:, k, :], identity[:])
+        turned = [
+            psum.tile([P, P], BF16, name="turned0", tag="bank"),
+            psum.tile([P, P], BF16, name="turned1"),
+        ]
         window = held.tile([P, S], BF16, name="window")
-        nc.vector.tensor_copy(window[:], turned[:])
+        for k in range(S // P):
+            nc.tensor.transpose(turned[k][:], rows[:, k, :], identity[:])
+        for k in range(S // P):
+            nc.vector.tensor_copy(window[:, k * P : (k + 1) * P], turned[k][:])
 
         cand_ps = [psum.tile([P, N], F32, name=f"cand_ps{k}") for k in range(H // P)]
-        mach_ps = [psum.tile([P, M], F32, name=f"mach_ps{k}") for k in range(H // P)]
+        mach_ps = [psum.tile([P, M], F32, name=f"mach_ps{k}", tag="bank") for k in range(H // P)]
         cand = [held.tile([P, N], F32, name=f"cand{k}") for k in range(H // P)]
         mach = [held.tile([P, M], F32, name=f"mach{k}") for k in range(H // P)]
         nc.tensor.matmul(mach_ps[0][:], wm_sb[:, 0:P], fm_sb[:])

@@ -22,10 +22,10 @@ def tile_learnablenetwork_kernel(tc, table, wj, fm, wm, b, offs, out):
         tc.psum_pool(name="psum", bufs=1) as psum,
     ):
         offsets = held.tile([P, N // 16], U16, name="offsets")
-        rows = held.tile([P, S // P, P], BF16, name="rows")
-        wj_sb = held.tile([P, H], BF16, name="wj_sb")
-        wm_sb = held.tile([P, H], BF16, name="wm_sb")
-        fm_sb = held.tile([P, M], BF16, name="fm_sb")
+        rows = held.tile([P, S // P, P], BF16, name="rows", align_bytes=256)
+        wj_sb = held.tile([P, H], BF16, name="wj_sb", align_bytes=256)
+        wm_sb = held.tile([P, H], BF16, name="wm_sb", align_bytes=256)
+        fm_sb = held.tile([P, M], BF16, name="fm_sb", align_bytes=256)
         for k in range(S // P):
             nc.sync.dma_start(rows[:, k, :], table[k * P : (k + 1) * P, :])
         nc.sync.dma_start(wm_sb[:], wm)
@@ -56,7 +56,8 @@ def tile_learnablenetwork_kernel(tc, table, wj, fm, wm, b, offs, out):
         for k in range(H // P):
             nc.tensor.matmul(cand_ps[k][:], wj_sb[:, k * P : (k + 1) * P], window[:].indirect(offsets[:]))
         nc.tensor.matmul(mach_ps[1][:], wm_sb[:, P : 2 * P], fm_sb[:])
-        nc.vector.tensor_scalar_add(cand[0][:], cand_ps[0][:], bias[0][:, 0:1])
+        for part in (slice(0, DIRECT), slice(DIRECT, N)):
+            nc.vector.tensor_scalar_add(cand[0][:, part], cand_ps[0][:, part], bias[0][:, 0:1])
         nc.vector.tensor_copy(mach[0][:], mach_ps[0][:])
 
         stores = 0

import concourse.mybir as mybir
from concourse.masks import make_identity

BF16, F32, U16 = mybir.dt.bfloat16, mybir.dt.float32, mybir.dt.uint16
TANH = mybir.ActivationFunctionType.Tanh

P = 128
S = 256
H = 256
N = 64
M = 128
DIRECT = 6

FLOPS = 2 * P * H * (N + M)


def tile_learnablenetwork_kernel(tc, table, wj, fm, wm, b, offs, out):
    nc = tc.nc
    with (
        tc.tile_pool(name="held", bufs=1) as held,
        tc.tile_pool(name="staged", bufs=1) as staged,
        tc.psum_pool(name="psum", bufs=1) as psum,
    ):
        offsets = held.tile([P, N // 16], U16, name="offsets")
        rows = held.tile([P, S // P, P], BF16, name="rows", align_bytes=256)
        wj_sb = held.tile([P, H], BF16, name="wj_sb", align_bytes=256)
        wm_sb = held.tile([P, H], BF16, name="wm_sb", align_bytes=256)
        fm_sb = held.tile([P, M], BF16, name="fm_sb", align_bytes=256)
        for k in range(S // P):
            nc.sync.dma_start(rows[:, k, :], table[k * P : (k + 1) * P, :])
        nc.sync.dma_start(wm_sb[:], wm)
        nc.sync.dma_start(fm_sb[:], fm)
        nc.sync.dma_start(offsets[:], offs)
        nc.sync.dma_start(wj_sb[:], wj)
        bias = [held.tile([P, 1], F32, name=f"bias{k}") for k in range(H // P)]
        for k in range(H // P):
            nc.sync.dma_start(bias[k][:], b[k * P : (k + 1) * P, :])

        identity = held.tile([P, P], BF16, name="identity")
        make_identity(nc, identity[:])
        turned = [
            psum.tile([P, P], BF16, name="turned0", tag="bank"),
            psum.tile([P, P], BF16, name="turned1"),
        ]
        window = held.tile([P, S], BF16, name="window")
        for k in range(S // P):
            nc.tensor.transpose(turned[k][:], rows[:, k, :], identity[:])
        for k in range(S // P):
            nc.vector.tensor_copy(window[:, k * P : (k + 1) * P], turned[k][:])

        cand_ps = [psum.tile([P, N], F32, name=f"cand_ps{k}") for k in range(H // P)]
        mach_ps = [psum.tile([P, M], F32, name=f"mach_ps{k}", tag="bank") for k in range(H // P)]
        cand = [held.tile([P, N], F32, name=f"cand{k}") for k in range(H // P)]
        mach = [held.tile([P, M], F32, name=f"mach{k}") for k in range(H // P)]
        nc.tensor.matmul(mach_ps[0][:], wm_sb[:, 0:P], fm_sb[:])
        for k in range(H // P):
            nc.tensor.matmul(cand_ps[k][:], wj_sb[:, k * P : (k + 1) * P], window[:].indirect(offsets[:]))
        nc.tensor.matmul(mach_ps[1][:], wm_sb[:, P : 2 * P], fm_sb[:])
        for part in (slice(0, DIRECT), slice(DIRECT, N)):
            nc.vector.tensor_scalar_add(cand[0][:, part], cand_ps[0][:, part], bias[0][:, 0:1])
        nc.vector.tensor_copy(mach[0][:], mach_ps[0][:])

        stores = 0
        for k in range(H // P):
            first = 0
            while first < N:
                count = min(1 + stores // 2, N - first)
                pairs = staged.tile([P, count * M], F32, name=f"pairs{k}_{first}", align_bytes=256)
                if k == 0:
                    for i in range(count):
                        j = first + i
                        one = pairs[:, i * M : (i + 1) * M]
                        if first < DIRECT:
                            nc.scalar.activation(one, mach_ps[k][:], TANH, bias=cand[k][:, j : j + 1])
                        else:
                            nc.vector.tensor_scalar_add(one, mach[k][:], cand[k][:, j : j + 1])
                else:
                    machines = mach[k][:].unsqueeze(1).to_broadcast([P, count, M])
                    candidates = cand[k][:, first : first + count].unsqueeze(2).to_broadcast([P, count, M])
                    nc.vector.tensor_add(pairs[:].rearrange("p (c m) -> p c m", m=M), machines, candidates)
                if not (k == 0 and first < DIRECT):
                    nc.scalar.activation(pairs[:], pairs[:], TANH)
                nc.sync.dma_start(out[k * P : (k + 1) * P, first * M : (first + count) * M], pairs[:])
                if k == 0 and first == DIRECT:
                    nc.vector.tensor_copy(mach[1][:], mach_ps[1][:])
                    nc.vector.tensor_scalar_add(cand[1][:], cand_ps[1][:], bias[1][:, 0:1])
                first += count
                stores += 1
